import numpy as np
import ml_dtypes


def mxq(x, axis, fmt="e4m3"):
    dtype, down = {"e4m3": (ml_dtypes.float8_e4m3fn, 7), "e5m2": (ml_dtypes.float8_e5m2, 14)}[fmt]
    v = np.moveaxis(np.asarray(x, np.float32).astype(ml_dtypes.bfloat16).astype(np.float64), axis, -1)
    blocks = v.reshape(v.shape[:-1] + (-1, 32))
    amax = np.abs(blocks).max(-1, keepdims=True)
    byte = np.maximum(np.where(amax > 0, np.frexp(amax)[1] - 1 + 127, 0) - down, 1)
    scale = np.exp2(byte - 127.0)
    codes = (blocks / scale).astype(np.float32).astype(dtype).astype(np.float64)
    return np.moveaxis((codes * scale).reshape(v.shape), -1, axis)


WIDE = False


def mx_kscale(k):
    if not WIDE:
        return np.ones(k)
    levels = np.array([10, -10, 5, -5, 0])
    a = np.random.permutation(np.resize(levels, k // 512 * 4)).reshape(k // 512, 4)
    idx = np.arange(k)
    return np.exp2(a[idx // 512, idx % 128 // 32])


BF16 = ml_dtypes.bfloat16


def bf(x):
    return np.asarray(x, np.float32).astype(BF16)


def f64(x):
    return np.asarray(x).astype(np.float64)


B, N, F, C0, C1, E, G = 4, 1024, 256, 2048, 1024, 2, 4
EPS_L1 = 1e-12


def setup_inputs():
    s = mx_kscale(N)
    return {"node_feat": bf(np.random.standard_normal((B, N, F)) * 5.0 * s.mean() / s[:, None]),
            "edge_feat": bf(np.random.uniform(-0.5, 1.0, (B, E, N, N)) * s)}


def reference(node_feat, edge_feat):
    diag_mask = 1.0 - np.eye(N)
    e = f64(edge_feat) * diag_mask[None, None, :, :]
    e = e / np.maximum(np.abs(e).sum(-1, keepdims=True), EPS_L1)
    e = e
    aggr = mxq(e, 3, "e4m3") @ mxq(f64(node_feat)[:, None, :, :], 2, "e4m3")
    return aggr.transpose(0, 2, 1, 3).reshape(B, N, E * F)

@@ -1,0 +1,191 @@
+import concourse.mybir as mybir
+from concourse.masks import make_identity
+
+BF16 = mybir.dt.bfloat16
+F32 = mybir.dt.float32
+U32 = mybir.dt.uint32
+U8 = mybir.dt.uint8
+FP8X4 = mybir.dt.float8_e4m3fn_x4
+ALU = mybir.AluOpType
+ACT = mybir.ActivationFunctionType
+
+P = 128
+GRAPHS = 4
+TYPES = 2
+NODES = 1024
+FEATS = 256
+EPS_L1 = 1e-12
+
+PACK = 4
+K_PASS = P * PACK
+PASSES = NODES // K_PASS
+PAIRS = PACK // 2
+WORDS = NODES // 2
+
+TILES_PER_GRAPH = NODES // P
+TILES = GRAPHS * TILES_PER_GRAPH
+
+FLOPS = 2 * GRAPHS * TYPES * NODES * NODES * FEATS
+
+EDGE_LOAD_LEAD = 6
+NODE_LOAD_LEAD = 5
+
+
+def tile_nodeupdatenetwork_pa_t_kernel(tc, node_feat, edge_feat, out):
+    nc = tc.nc
+
+    with tc.tile_pool(name="const", bufs=1) as const, tc.tile_pool(
+        name="edges", bufs=EDGE_LOAD_LEAD + 2
+    ) as edges, tc.tile_pool(name="work", bufs=3) as work, tc.tile_pool(
+        name="nodes", bufs=2
+    ) as nodes, tc.psum_pool(name="turned", bufs=4) as turned, tc.psum_pool(
+        name="sums", bufs=3
+    ) as sums:
+        identity = const.tile([P, P], F32)
+        make_identity(nc, identity[:])
+        off_diagonal = const.tile([P, P], BF16)
+        nc.vector.tensor_scalar(
+            out=off_diagonal[:], in0=identity[:], scalar1=-1.0, scalar2=1.0, op0=ALU.mult, op1=ALU.add
+        )
+
+        m_of, l1_of, inv_of, w_of, turned_of, grouped_of = {}, {}, {}, {}, {}, {}
+        codes_of, scales_of, acc_of = {}, {}, {}
+        x_raw_of, x_grouped_of, x_codes_of, x_scales_of = {}, {}, {}, {}
+
+        def graph_and_rows(t):
+            first = (t % TILES_PER_GRAPH) * P
+            return t // TILES_PER_GRAPH, first
+
+        def load_nodes(b):
+            x_raw = nodes.tile([P, PASSES * PACK * FEATS], BF16, name="x_raw")
+            nc.sync.dma_start(
+                out=x_raw[:].rearrange("p (c r) -> p c r", r=2 * FEATS),
+                in_=node_feat[b].rearrange("(c p h) f -> p c (h f)", p=P, h=2),
+            )
+            x_raw_of[b] = x_raw
+
+        def group_nodes(b):
+            x_grouped = nodes.tile([P, PASSES * FEATS * PACK], BF16, name="x_grouped", align_bytes=64)
+            src = x_raw_of[b][:].rearrange("p (g t f) -> p g t f", g=PASSES, t=PACK)
+            dst = x_grouped[:].rearrange("p (g f t) -> p g f t", g=PASSES, t=PACK)
+            for g in range(PASSES):
+                nc.vector.tensor_copy(out=dst[:, g], in_=src[:, g].rearrange("p t f -> p f t"))
+            x_grouped_of[b] = x_grouped
+
+        def quantise_nodes(b):
+            x_codes = nodes.tile([P, PASSES * FEATS], U32, name="x_codes", align_bytes=64)
+            x_scales = nodes.tile([P, PASSES * FEATS], U8, name="x_scales", align_bytes=64)
+            nc.vector.quantize_mx(out=x_codes[:].bitcast(FP8X4), scales=x_scales[:], in_=x_grouped_of[b][:])
+            x_codes_of[b], x_scales_of[b] = x_codes, x_scales
+
+        def load_edges(t):
+            b, first = graph_and_rows(t)
+            m = edges.tile([P, TYPES, NODES], BF16, name="m")
+            nc.sync.dma_start(out=m[:], in_=edge_feat[b, :, first : first + P, :].rearrange("e p k -> p e k"))
+            m_of[t] = m
+
+        def mask_self_edges(t):
+            b, first = graph_and_rows(t)
+            block = m_of[t][:, :, first : first + P]
+            nc.vector.tensor_tensor(
+                out=block, in0=block, in1=off_diagonal[:].unsqueeze(1).to_broadcast([P, TYPES, P]), op=ALU.mult
+            )
+
+        def sum_absolute(t):
+            l1 = work.tile([P, TYPES], F32, name="l1")
+            for e in range(TYPES):
+                unread = work.tile([P, NODES], BF16, name="unread", bufs=4)
+                nc.scalar.activation(out=unread[:], in_=m_of[t][:, e, :], func=ACT.Abs, accum_out=l1[:, e : e + 1])
+            l1_of[t] = l1
+
+        def clamp_sums(t):
+            inv = work.tile([P, TYPES], F32, name="inv")
+            nc.vector.tensor_scalar(out=inv[:], in0=l1_of[t][:], scalar1=EPS_L1, scalar2=None, op0=ALU.max)
+            inv_of[t] = inv
+
+        def invert_sums(t):
+            nc.vector.reciprocal(out=inv_of[t][:], in_=inv_of[t][:])
+
+        def normalise(t):
+            w = work.tile([P, TYPES * NODES], BF16, name="w")
+            for e in range(TYPES):
+                nc.vector.tensor_scalar(
+                    out=w[:, e * NODES : (e + 1) * NODES],
+                    in0=m_of[t][:, e, :],
+                    scalar1=inv_of[t][:, e : e + 1],
+                    scalar2=None,
+                    op0=ALU.mult,
+                )
+            w_of[t] = w
+
+        def transpose(t):
+            words = w_of[t][:].bitcast(F32)
+            for e in range(TYPES):
+                w_t = turned.tile([P, WORDS], F32, name="w_t")
+                for q in range(WORDS // P):
+                    first = e * WORDS + q * P
+                    nc.tensor.transpose(w_t[:, q * P : (q + 1) * P], words[:, first : first + P], identity[:])
+                turned_of[t, e] = w_t
+
+        def group(t, e):
+            if e == 0:
+                grouped_of[t] = work.tile([P, TYPES * PASSES * P * PACK], BF16, name="grouped", align_bytes=64)
+            dst = grouped_of[t][:].bitcast(F32).rearrange("p (e g n u) -> p e g n u", e=TYPES, g=PASSES, u=PAIRS)
+            src = turned_of[t, e][:].rearrange("p (g u n) -> p g n u", g=PASSES, u=PAIRS)
+            nc.vector.tensor_copy(out=dst[:, e], in_=src)
+
+        def quantise(t):
+            codes = work.tile([P, TYPES * PASSES * P], U32, name="codes", align_bytes=64)
+            scales = work.tile([P, TYPES * PASSES * P], U8, name="scales", align_bytes=64)
+            nc.vector.quantize_mx(out=codes[:].bitcast(FP8X4), scales=scales[:], in_=grouped_of[t][:])
+            codes_of[t], scales_of[t] = codes, scales
+
+        def multiply(t):
+            b, first = graph_and_rows(t)
+            acc = sums.tile([P, TYPES * FEATS], F32, name="acc")
+            for e in range(TYPES):
+                for g in range(PASSES):
+                    n_cols = slice((e * PASSES + g) * P, (e * PASSES + g + 1) * P)
+                    f_cols = slice(g * FEATS, (g + 1) * FEATS)
+                    nc.tensor.matmul_mx(
+                        out=acc[:, e * FEATS : (e + 1) * FEATS],
+                        lhsT=codes_of[t][:, n_cols].bitcast(FP8X4),
+                        lhsT_scale=scales_of[t][:, n_cols],
+                        rhs=x_codes_of[b][:, f_cols].bitcast(FP8X4),
+                        rhs_scale=x_scales_of[b][:, f_cols],
+                        start=(g == 0),
+                        stop=(g == PASSES - 1),
+                    )
+            acc_of[t] = acc
+
+        def store(t):
+            b, first = graph_and_rows(t)
+            result = work.tile([P, TYPES * FEATS], F32, name="result")
+            nc.scalar.copy(out=result[:], in_=acc_of[t][:])
+            nc.sync.dma_start(out=out[b, first : first + P, :], in_=result[:])
+
+        def for_tile(t, stage):
+            if 0 <= t < TILES:
+                stage(t)
+
+        def for_graph_starting_at(t, stage):
+            if 0 <= t < TILES and t % TILES_PER_GRAPH == 0:
+                stage(t // TILES_PER_GRAPH)
+
+        with tc.manual_schedule():
+            for step in range(-EDGE_LOAD_LEAD, TILES + 4):
+                for_tile(step + EDGE_LOAD_LEAD, load_edges)
+                for_graph_starting_at(step + NODE_LOAD_LEAD, load_nodes)
+                for_tile(step, sum_absolute)
+                for_tile(step - 1, clamp_sums)
+                for_tile(step - 2, lambda t: group(t, 0))
+                for_tile(step - 1, invert_sums)
+                for_tile(step - 2, lambda t: group(t, 1))
+                for_tile(step - 1, normalise)
+                for_tile(step - 1, transpose)
+                for_tile(step - 2, quantise)
+                for_tile(step - 2, multiply)
+                for_tile(step + 1, mask_self_edges)
+                for_graph_starting_at(step, quantise_nodes)
+                for_graph_starting_at(step + 1, group_nodes)
+                for_tile(step - 3, store)

@@ -27,8 +27,12 @@ TILES = GRAPHS * TILES_PER_GRAPH
 
 FLOPS = 2 * GRAPHS * TYPES * NODES * NODES * FEATS
 
-EDGE_LOAD_LEAD = 6
-NODE_LOAD_LEAD = 5
+SUM_LEAD = 3
+MASK_LEAD = SUM_LEAD + 2
+EDGE_LOAD_LEAD = MASK_LEAD + 3
+NODE_LOAD_LEAD = EDGE_LOAD_LEAD - 2
+STORE_LAG = 4
+VECTOR_SHARE = 3
 
 
 def tile_nodeupdatenetwork_pa_t_kernel(tc, node_feat, edge_feat, out):
@@ -39,14 +43,13 @@ def tile_nodeupdatenetwork_pa_t_kernel(tc, node_feat, edge_feat, out):
     ) as edges, tc.tile_pool(name="work", bufs=3) as work, tc.tile_pool(
         name="nodes", bufs=2
     ) as nodes, tc.psum_pool(name="turned", bufs=4) as turned, tc.psum_pool(
-        name="sums", bufs=3
+        name="sums", bufs=4
     ) as sums:
         identity = const.tile([P, P], F32)
         make_identity(nc, identity[:])
-        off_diagonal = const.tile([P, P], BF16)
-        nc.vector.tensor_scalar(
-            out=off_diagonal[:], in0=identity[:], scalar1=-1.0, scalar2=1.0, op0=ALU.mult, op1=ALU.add
-        )
+
+        table_warmer = const.tile([P, 1], F32)
+        nc.scalar.activation(out=table_warmer[:], in_=identity[:, 0:1], func=ACT.Abs)
 
         m_of, l1_of, inv_of, w_of, turned_of, grouped_of = {}, {}, {}, {}, {}, {}
         codes_of, scales_of, acc_of = {}, {}, {}
@@ -86,13 +89,20 @@ def tile_nodeupdatenetwork_pa_t_kernel(tc, node_feat, edge_feat, out):
 
         def mask_self_edges(t):
             b, first = graph_and_rows(t)
-            block = m_of[t][:, :, first : first + P]
-            nc.vector.tensor_tensor(
-                out=block, in0=block, in1=off_diagonal[:].unsqueeze(1).to_broadcast([P, TYPES, P]), op=ALU.mult
-            )
+            for e in range(TYPES):
+                block = m_of[t][:, e, first : first + P]
+                nc.gpsimd.affine_select(
+                    out=block,
+                    in_=block,
+                    pattern=[[-1, P]],
+                    compare_op=ALU.not_equal,
+                    fill=0.0,
+                    base=0,
+                    channel_multiplier=1,
+                )
 
         def sum_absolute(t):
-            l1 = work.tile([P, TYPES], F32, name="l1")
+            l1 = work.tile([P, TYPES], F32, name="l1", bufs=SUM_LEAD + 3)
             for e in range(TYPES):
                 unread = work.tile([P, NODES], BF16, name="unread", bufs=4)
                 nc.scalar.activation(out=unread[:], in_=m_of[t][:, e, :], func=ACT.Abs, accum_out=l1[:, e : e + 1])
@@ -161,7 +171,10 @@ def tile_nodeupdatenetwork_pa_t_kernel(tc, node_feat, edge_feat, out):
         def store(t):
             b, first = graph_and_rows(t)
             result = work.tile([P, TYPES * FEATS], F32, name="result")
-            nc.scalar.copy(out=result[:], in_=acc_of[t][:])
+            if t % VECTOR_SHARE == VECTOR_SHARE - 1:
+                nc.vector.tensor_copy(out=result[:], in_=acc_of[t][:])
+            else:
+                nc.scalar.copy(out=result[:], in_=acc_of[t][:])
             nc.sync.dma_start(out=out[b, first : first + P, :], in_=result[:])
 
         def for_tile(t, stage):
@@ -173,19 +186,19 @@ def tile_nodeupdatenetwork_pa_t_kernel(tc, node_feat, edge_feat, out):
                 stage(t // TILES_PER_GRAPH)
 
         with tc.manual_schedule():
-            for step in range(-EDGE_LOAD_LEAD, TILES + 4):
+            for step in range(-EDGE_LOAD_LEAD, TILES + STORE_LAG + 1):
                 for_tile(step + EDGE_LOAD_LEAD, load_edges)
                 for_graph_starting_at(step + NODE_LOAD_LEAD, load_nodes)
-                for_tile(step, sum_absolute)
-                for_tile(step - 1, clamp_sums)
-                for_tile(step - 2, lambda t: group(t, 0))
-                for_tile(step - 1, invert_sums)
-                for_tile(step - 2, lambda t: group(t, 1))
+                for_tile(step + SUM_LEAD, sum_absolute)
                 for_tile(step - 1, normalise)
                 for_tile(step - 1, transpose)
-                for_tile(step - 2, quantise)
-                for_tile(step - 2, multiply)
-                for_tile(step + 1, mask_self_edges)
-                for_graph_starting_at(step, quantise_nodes)
-                for_graph_starting_at(step + 1, group_nodes)
-                for_tile(step - 3, store)
+                for_tile(step - 3, quantise)
+                for_tile(step - 3, multiply)
+                for_tile(step, clamp_sums)
+                for_tile(step + MASK_LEAD, mask_self_edges)
+                for_tile(step - 2, lambda t: group(t, 0))
+                for_tile(step, invert_sums)
+                for_tile(step - 2, lambda t: group(t, 1))
+                for_tile(step - STORE_LAG, store)
+                for_graph_starting_at(step - 2, quantise_nodes)
+                for_graph_starting_at(step - 1, group_nodes)

@@ -5,6 +5,7 @@ BF16 = mybir.dt.bfloat16
 F32 = mybir.dt.float32
 U32 = mybir.dt.uint32
 U8 = mybir.dt.uint8
+I32 = mybir.dt.int32
 FP8X4 = mybir.dt.float8_e4m3fn_x4
 ALU = mybir.AluOpType
 ACT = mybir.ActivationFunctionType
@@ -15,7 +16,9 @@ TYPES = 2
 NODES = 1024
 FEATS = 256
 EPS_L1 = 1e-12
+CLEAR_SIGNS = 0x7FFF7FFF
 
+SUM_PITCH = 8
 PACK = 4
 K_PASS = P * PACK
 PASSES = NODES // K_PASS
@@ -27,12 +30,12 @@ TILES = GRAPHS * TILES_PER_GRAPH
 
 FLOPS = 2 * GRAPHS * TYPES * NODES * NODES * FEATS
 
-SUM_LEAD = 3
+SUM_LEAD = 2
 MASK_LEAD = SUM_LEAD + 2
 EDGE_LOAD_LEAD = MASK_LEAD + 3
 NODE_LOAD_LEAD = EDGE_LOAD_LEAD - 2
 STORE_LAG = 4
-VECTOR_SHARE = 3
+VECTOR_SHARE = 4
 
 
 def tile_nodeupdatenetwork_pa_t_kernel(tc, node_feat, edge_feat, out):
@@ -51,7 +54,7 @@ def tile_nodeupdatenetwork_pa_t_kernel(tc, node_feat, edge_feat, out):
         table_warmer = const.tile([P, 1], F32)
         nc.scalar.activation(out=table_warmer[:], in_=identity[:, 0:1], func=ACT.Abs)
 
-        m_of, l1_of, inv_of, w_of, turned_of, grouped_of = {}, {}, {}, {}, {}, {}
+        m_of, l1_of, magnitude_of, inv_of, w_of, turned_of, grouped_of = {}, {}, {}, {}, {}, {}, {}
         codes_of, scales_of, acc_of = {}, {}, {}
         x_raw_of, x_grouped_of, x_codes_of, x_scales_of = {}, {}, {}, {}
 
@@ -101,32 +104,53 @@ def tile_nodeupdatenetwork_pa_t_kernel(tc, node_feat, edge_feat, out):
                     channel_multiplier=1,
                 )
 
-        def sum_absolute(t):
-            l1 = work.tile([P, TYPES], F32, name="l1", bufs=SUM_LEAD + 3)
-            for e in range(TYPES):
-                unread = work.tile([P, NODES], BF16, name="unread", bufs=4)
-                nc.scalar.activation(out=unread[:], in_=m_of[t][:, e, :], func=ACT.Abs, accum_out=l1[:, e : e + 1])
+        def sum_type_0(t):
+            l1 = work.tile([P, TYPES, SUM_PITCH], F32, name="l1", bufs=SUM_LEAD + 3)
+            unread = work.tile([P, NODES], BF16, name="unread", bufs=4)
+            nc.scalar.activation(out=unread[:], in_=m_of[t][:, 0, :], func=ACT.Abs, accum_out=l1[:, 0, 0:1])
             l1_of[t] = l1
+
+        def magnitude_type_1(t):
+            magnitude = work.tile([P, NODES], BF16, name="magnitude")
+            nc.vector.tensor_scalar(
+                out=magnitude[:].bitcast(I32),
+                in0=m_of[t][:, 1, :].bitcast(I32),
+                scalar1=CLEAR_SIGNS,
+                scalar2=None,
+                op0=ALU.bitwise_and,
+            )
+            magnitude_of[t] = magnitude
+
+        def sum_type_1(t):
+            unread = work.tile([P, NODES], BF16, name="unread_too")
+            nc.vector.tensor_scalar(
+                out=unread[:],
+                in0=magnitude_of[t][:],
+                scalar1=1.0,
+                scalar2=None,
+                op0=ALU.mult,
+                op1=ALU.add,
+                accum_out=l1_of[t][:, 1, 0:1],
+            )
 
         def clamp_sums(t):
             inv = work.tile([P, TYPES], F32, name="inv")
-            nc.vector.tensor_scalar(out=inv[:], in0=l1_of[t][:], scalar1=EPS_L1, scalar2=None, op0=ALU.max)
+            nc.vector.tensor_scalar(out=inv[:], in0=l1_of[t][:, :, 0], scalar1=EPS_L1, scalar2=None, op0=ALU.max)
             inv_of[t] = inv
 
         def invert_sums(t):
             nc.vector.reciprocal(out=inv_of[t][:], in_=inv_of[t][:])
 
-        def normalise(t):
-            w = work.tile([P, TYPES * NODES], BF16, name="w")
-            for e in range(TYPES):
-                nc.vector.tensor_scalar(
-                    out=w[:, e * NODES : (e + 1) * NODES],
-                    in0=m_of[t][:, e, :],
-                    scalar1=inv_of[t][:, e : e + 1],
-                    scalar2=None,
-                    op0=ALU.mult,
-                )
-            w_of[t] = w
+        def normalise(t, e):
+            if e == 0:
+                w_of[t] = work.tile([P, TYPES * NODES], BF16, name="w")
+            nc.vector.tensor_scalar(
+                out=w_of[t][:, e * NODES : (e + 1) * NODES],
+                in0=m_of[t][:, e, :],
+                scalar1=inv_of[t][:, e : e + 1],
+                scalar2=None,
+                op0=ALU.mult,
+            )
 
         def transpose(t):
             words = w_of[t][:].bitcast(F32)
@@ -142,7 +166,7 @@ def tile_nodeupdatenetwork_pa_t_kernel(tc, node_feat, edge_feat, out):
                 grouped_of[t] = work.tile([P, TYPES * PASSES * P * PACK], BF16, name="grouped", align_bytes=64)
             dst = grouped_of[t][:].bitcast(F32).rearrange("p (e g n u) -> p e g n u", e=TYPES, g=PASSES, u=PAIRS)
             src = turned_of[t, e][:].rearrange("p (g u n) -> p g n u", g=PASSES, u=PAIRS)
-            nc.vector.tensor_copy(out=dst[:, e], in_=src)
+            nc.scalar.copy(out=dst[:, e], in_=src)
 
         def quantise(t):
             codes = work.tile([P, TYPES * PASSES * P], U32, name="codes", align_bytes=64)
@@ -189,15 +213,18 @@ def tile_nodeupdatenetwork_pa_t_kernel(tc, node_feat, edge_feat, out):
             for step in range(-EDGE_LOAD_LEAD, TILES + STORE_LAG + 1):
                 for_tile(step + EDGE_LOAD_LEAD, load_edges)
                 for_graph_starting_at(step + NODE_LOAD_LEAD, load_nodes)
-                for_tile(step + SUM_LEAD, sum_absolute)
-                for_tile(step - 1, normalise)
+                for_tile(step + MASK_LEAD, mask_self_edges)
+                for_tile(step + SUM_LEAD, sum_type_0)
+                for_tile(step, magnitude_type_1)
+                for_tile(step - 1, lambda t: normalise(t, 0))
+                for_tile(step, sum_type_1)
+                for_tile(step - 1, lambda t: normalise(t, 1))
                 for_tile(step - 1, transpose)
+                for_tile(step, clamp_sums)
                 for_tile(step - 3, quantise)
                 for_tile(step - 3, multiply)
-                for_tile(step, clamp_sums)
-                for_tile(step + MASK_LEAD, mask_self_edges)
-                for_tile(step - 2, lambda t: group(t, 0))
                 for_tile(step, invert_sums)
+                for_tile(step - 2, lambda t: group(t, 0))
                 for_tile(step - 2, lambda t: group(t, 1))
                 for_tile(step - STORE_LAG, store)
                 for_graph_starting_at(step - 2, quantise_nodes)

@@ -35,7 +35,7 @@ MASK_LEAD = SUM_LEAD + 2
 EDGE_LOAD_LEAD = MASK_LEAD + 3
 NODE_LOAD_LEAD = EDGE_LOAD_LEAD - 2
 STORE_LAG = 4
-VECTOR_SHARE = 4
+VECTOR_SHARE = 2
 
 
 def tile_nodeupdatenetwork_pa_t_kernel(tc, node_feat, edge_feat, out):
@@ -87,7 +87,8 @@ def tile_nodeupdatenetwork_pa_t_kernel(tc, node_feat, edge_feat, out):
         def load_edges(t):
             b, first = graph_and_rows(t)
             m = edges.tile([P, TYPES, NODES], BF16, name="m")
-            nc.sync.dma_start(out=m[:], in_=edge_feat[b, :, first : first + P, :].rearrange("e p k -> p e k"))
+            for e in range(TYPES):
+                nc.sync.dma_start(out=m[:, e, :], in_=edge_feat[b, e, first : first + P, :])
             m_of[t] = m
 
         def mask_self_edges(t):

@@ -34,8 +34,8 @@ SUM_LEAD = 2
 MASK_LEAD = SUM_LEAD + 2
 EDGE_LOAD_LEAD = MASK_LEAD + 3
 NODE_LOAD_LEAD = EDGE_LOAD_LEAD - 2
-STORE_LAG = 4
-VECTOR_SHARE = 2
+STORE_LAG = 6
+VECTOR_SHARE = 3
 
 
 def tile_nodeupdatenetwork_pa_t_kernel(tc, node_feat, edge_feat, out):
@@ -72,10 +72,10 @@ def tile_nodeupdatenetwork_pa_t_kernel(tc, node_feat, edge_feat, out):
 
         def group_nodes(b):
             x_grouped = nodes.tile([P, PASSES * FEATS * PACK], BF16, name="x_grouped", align_bytes=64)
-            src = x_raw_of[b][:].rearrange("p (g t f) -> p g t f", g=PASSES, t=PACK)
-            dst = x_grouped[:].rearrange("p (g f t) -> p g f t", g=PASSES, t=PACK)
+            src = x_raw_of[b][:].rearrange("p (g j c i) -> p g c j i", g=PASSES, j=PACK, i=4)
+            dst = x_grouped[:].rearrange("p (g c i j) -> p g c j i", g=PASSES, j=PACK, i=4)
             for g in range(PASSES):
-                nc.vector.tensor_copy(out=dst[:, g], in_=src[:, g].rearrange("p t f -> p f t"))
+                nc.vector.tensor_copy(out=dst[:, g], in_=src[:, g])
             x_grouped_of[b] = x_grouped
 
         def quantise_nodes(b):
@@ -87,8 +87,7 @@ def tile_nodeupdatenetwork_pa_t_kernel(tc, node_feat, edge_feat, out):
         def load_edges(t):
             b, first = graph_and_rows(t)
             m = edges.tile([P, TYPES, NODES], BF16, name="m")
-            for e in range(TYPES):
-                nc.sync.dma_start(out=m[:, e, :], in_=edge_feat[b, e, first : first + P, :])
+            nc.sync.dma_start(out=m[:], in_=edge_feat[b, :, first : first + P, :].rearrange("e p k -> p e k"))
             m_of[t] = m
 
         def mask_self_edges(t):

import concourse.mybir as mybir
from concourse.masks import make_identity

BF16 = mybir.dt.bfloat16
F32 = mybir.dt.float32
U32 = mybir.dt.uint32
U8 = mybir.dt.uint8
I32 = mybir.dt.int32
FP8X4 = mybir.dt.float8_e4m3fn_x4
ALU = mybir.AluOpType
ACT = mybir.ActivationFunctionType

P = 128
GRAPHS = 4
TYPES = 2
NODES = 1024
FEATS = 256
EPS_L1 = 1e-12
CLEAR_SIGNS = 0x7FFF7FFF

SUM_PITCH = 8
PACK = 4
K_PASS = P * PACK
PASSES = NODES // K_PASS
PAIRS = PACK // 2
WORDS = NODES // 2

TILES_PER_GRAPH = NODES // P
TILES = GRAPHS * TILES_PER_GRAPH

FLOPS = 2 * GRAPHS * TYPES * NODES * NODES * FEATS

SUM_LEAD = 2
MASK_LEAD = SUM_LEAD + 2
EDGE_LOAD_LEAD = MASK_LEAD + 3
NODE_LOAD_LEAD = EDGE_LOAD_LEAD - 2
STORE_LAG = 6
VECTOR_SHARE = 3


def tile_nodeupdatenetwork_pa_t_kernel(tc, node_feat, edge_feat, out):
    nc = tc.nc

    with tc.tile_pool(name="const", bufs=1) as const, tc.tile_pool(
        name="edges", bufs=EDGE_LOAD_LEAD + 2
    ) as edges, tc.tile_pool(name="work", bufs=3) as work, tc.tile_pool(
        name="nodes", bufs=2
    ) as nodes, tc.psum_pool(name="turned", bufs=4) as turned, tc.psum_pool(
        name="sums", bufs=4
    ) as sums:
        identity = const.tile([P, P], F32)
        make_identity(nc, identity[:])

        table_warmer = const.tile([P, 1], F32)
        nc.scalar.activation(out=table_warmer[:], in_=identity[:, 0:1], func=ACT.Abs)

        m_of, l1_of, magnitude_of, inv_of, w_of, turned_of, grouped_of = {}, {}, {}, {}, {}, {}, {}
        codes_of, scales_of, acc_of = {}, {}, {}
        x_raw_of, x_grouped_of, x_codes_of, x_scales_of = {}, {}, {}, {}

        def graph_and_rows(t):
            first = (t % TILES_PER_GRAPH) * P
            return t // TILES_PER_GRAPH, first

        def load_nodes(b):
            x_raw = nodes.tile([P, PASSES * PACK * FEATS], BF16, name="x_raw")
            nc.sync.dma_start(
                out=x_raw[:].rearrange("p (c r) -> p c r", r=2 * FEATS),
                in_=node_feat[b].rearrange("(c p h) f -> p c (h f)", p=P, h=2),
            )
            x_raw_of[b] = x_raw

        def group_nodes(b):
            x_grouped = nodes.tile([P, PASSES * FEATS * PACK], BF16, name="x_grouped", align_bytes=64)
            src = x_raw_of[b][:].rearrange("p (g j c i) -> p g c j i", g=PASSES, j=PACK, i=4)
            dst = x_grouped[:].rearrange("p (g c i j) -> p g c j i", g=PASSES, j=PACK, i=4)
            for g in range(PASSES):
                nc.vector.tensor_copy(out=dst[:, g], in_=src[:, g])
            x_grouped_of[b] = x_grouped

        def quantise_nodes(b):
            x_codes = nodes.tile([P, PASSES * FEATS], U32, name="x_codes", align_bytes=64)
            x_scales = nodes.tile([P, PASSES * FEATS], U8, name="x_scales", align_bytes=64)
            nc.vector.quantize_mx(out=x_codes[:].bitcast(FP8X4), scales=x_scales[:], in_=x_grouped_of[b][:])
            x_codes_of[b], x_scales_of[b] = x_codes, x_scales

        def load_edges(t):
            b, first = graph_and_rows(t)
            m = edges.tile([P, TYPES, NODES], BF16, name="m")
            nc.sync.dma_start(out=m[:], in_=edge_feat[b, :, first : first + P, :].rearrange("e p k -> p e k"))
            m_of[t] = m

        def mask_self_edges(t):
            b, first = graph_and_rows(t)
            for e in range(TYPES):
                block = m_of[t][:, e, first : first + P]
                nc.gpsimd.affine_select(
                    out=block,
                    in_=block,
                    pattern=[[-1, P]],
                    compare_op=ALU.not_equal,
                    fill=0.0,
                    base=0,
                    channel_multiplier=1,
                )

        def sum_type_0(t):
            l1 = work.tile([P, TYPES, SUM_PITCH], F32, name="l1", bufs=SUM_LEAD + 3)
            unread = work.tile([P, NODES], BF16, name="unread", bufs=4)
            nc.scalar.activation(out=unread[:], in_=m_of[t][:, 0, :], func=ACT.Abs, accum_out=l1[:, 0, 0:1])
            l1_of[t] = l1

        def magnitude_type_1(t):
            magnitude = work.tile([P, NODES], BF16, name="magnitude")
            nc.vector.tensor_scalar(
                out=magnitude[:].bitcast(I32),
                in0=m_of[t][:, 1, :].bitcast(I32),
                scalar1=CLEAR_SIGNS,
                scalar2=None,
                op0=ALU.bitwise_and,
            )
            magnitude_of[t] = magnitude

        def sum_type_1(t):
            unread = work.tile([P, NODES], BF16, name="unread_too")
            nc.vector.tensor_scalar(
                out=unread[:],
                in0=magnitude_of[t][:],
                scalar1=1.0,
                scalar2=None,
                op0=ALU.mult,
                op1=ALU.add,
                accum_out=l1_of[t][:, 1, 0:1],
            )

        def clamp_sums(t):
            inv = work.tile([P, TYPES], F32, name="inv")
            nc.vector.tensor_scalar(out=inv[:], in0=l1_of[t][:, :, 0], scalar1=EPS_L1, scalar2=None, op0=ALU.max)
            inv_of[t] = inv

        def invert_sums(t):
            nc.vector.reciprocal(out=inv_of[t][:], in_=inv_of[t][:])

        def normalise(t, e):
            if e == 0:
                w_of[t] = work.tile([P, TYPES * NODES], BF16, name="w")
            nc.vector.tensor_scalar(
                out=w_of[t][:, e * NODES : (e + 1) * NODES],
                in0=m_of[t][:, e, :],
                scalar1=inv_of[t][:, e : e + 1],
                scalar2=None,
                op0=ALU.mult,
            )

        def transpose(t):
            words = w_of[t][:].bitcast(F32)
            for e in range(TYPES):
                w_t = turned.tile([P, WORDS], F32, name="w_t")
                for q in range(WORDS // P):
                    first = e * WORDS + q * P
                    nc.tensor.transpose(w_t[:, q * P : (q + 1) * P], words[:, first : first + P], identity[:])
                turned_of[t, e] = w_t

        def group(t, e):
            if e == 0:
                grouped_of[t] = work.tile([P, TYPES * PASSES * P * PACK], BF16, name="grouped", align_bytes=64)
            dst = grouped_of[t][:].bitcast(F32).rearrange("p (e g n u) -> p e g n u", e=TYPES, g=PASSES, u=PAIRS)
            src = turned_of[t, e][:].rearrange("p (g u n) -> p g n u", g=PASSES, u=PAIRS)
            nc.scalar.copy(out=dst[:, e], in_=src)

        def quantise(t):
            codes = work.tile([P, TYPES * PASSES * P], U32, name="codes", align_bytes=64)
            scales = work.tile([P, TYPES * PASSES * P], U8, name="scales", align_bytes=64)
            nc.vector.quantize_mx(out=codes[:].bitcast(FP8X4), scales=scales[:], in_=grouped_of[t][:])
            codes_of[t], scales_of[t] = codes, scales

        def multiply(t):
            b, first = graph_and_rows(t)
            acc = sums.tile([P, TYPES * FEATS], F32, name="acc")
            for e in range(TYPES):
                for g in range(PASSES):
                    n_cols = slice((e * PASSES + g) * P, (e * PASSES + g + 1) * P)
                    f_cols = slice(g * FEATS, (g + 1) * FEATS)
                    nc.tensor.matmul_mx(
                        out=acc[:, e * FEATS : (e + 1) * FEATS],
                        lhsT=codes_of[t][:, n_cols].bitcast(FP8X4),
                        lhsT_scale=scales_of[t][:, n_cols],
                        rhs=x_codes_of[b][:, f_cols].bitcast(FP8X4),
                        rhs_scale=x_scales_of[b][:, f_cols],
                        start=(g == 0),
                        stop=(g == PASSES - 1),
                    )
            acc_of[t] = acc

        def store(t):
            b, first = graph_and_rows(t)
            result = work.tile([P, TYPES * FEATS], F32, name="result")
            if t % VECTOR_SHARE == VECTOR_SHARE - 1:
                nc.vector.tensor_copy(out=result[:], in_=acc_of[t][:])
            else:
                nc.scalar.copy(out=result[:], in_=acc_of[t][:])
            nc.sync.dma_start(out=out[b, first : first + P, :], in_=result[:])

        def for_tile(t, stage):
            if 0 <= t < TILES:
                stage(t)

        def for_graph_starting_at(t, stage):
            if 0 <= t < TILES and t % TILES_PER_GRAPH == 0:
                stage(t // TILES_PER_GRAPH)

        with tc.manual_schedule():
            for step in range(-EDGE_LOAD_LEAD, TILES + STORE_LAG + 1):
                for_tile(step + EDGE_LOAD_LEAD, load_edges)
                for_graph_starting_at(step + NODE_LOAD_LEAD, load_nodes)
                for_tile(step + MASK_LEAD, mask_self_edges)
                for_tile(step + SUM_LEAD, sum_type_0)
                for_tile(step, magnitude_type_1)
                for_tile(step - 1, lambda t: normalise(t, 0))
                for_tile(step, sum_type_1)
                for_tile(step - 1, lambda t: normalise(t, 1))
                for_tile(step - 1, transpose)
                for_tile(step, clamp_sums)
                for_tile(step - 3, quantise)
                for_tile(step - 3, multiply)
                for_tile(step, invert_sums)
                for_tile(step - 2, lambda t: group(t, 0))
                for_tile(step - 2, lambda t: group(t, 1))
                for_tile(step - STORE_LAG, store)
                for_graph_starting_at(step - 2, quantise_nodes)
                for_graph_starting_at(step - 1, group_nodes)
